import numpy as np
import ml_dtypes

BF16 = ml_dtypes.bfloat16


def bf(x):
    return np.asarray(x, np.float32).astype(BF16)


def f32(x):
    return np.asarray(x, np.float32)


def f64(x):
    return np.asarray(x).astype(np.float64)


def striped(idx):
    return np.tile(idx.reshape(-1, 16).T, (8, 1))


C, S, B, L, N = 256, 4096, 8, 128, 1024


def smooth(x):
    e = x.reshape(C, B, L)
    s = e.copy()
    s[:, :, :-1] += e[:, :, 1:]
    s[:, :, 1:] += e[:, :, :-1]
    counts = np.full(L, 3.0)
    counts[0] = 2.0
    counts[-1] = 2.0
    return (s / counts + e).reshape(C, N)


def setup_inputs():
    return {"base": f32(np.random.standard_normal((C, S))), "x": f32(np.random.standard_normal((C, N))), "offs": striped(np.random.permutation(S)[:N])}


def reference(base, x, offs):
    idx = offs[:16].T.reshape(-1)
    out = f64(base).copy()
    out[:, idx] = smooth(f64(x))
    return out

@@ -1,0 +1,52 @@
+import concourse.mybir as mybir
+
+F32 = mybir.dt.float32
+U16 = mybir.dt.uint16
+ADD = mybir.AluOpType.add
+MULT = mybir.AluOpType.mult
+
+P = 128
+CHANNELS, SLOTS = 256, 4096
+SENTENCES, LENGTH = 8, 128
+TOKENS = SENTENCES * LENGTH
+
+
+def by_sentence(flat):
+    return flat.rearrange("p (s t) -> p s t", t=LENGTH)
+
+
+def tile_synalign_kernel(tc, base, x, offs, out):
+    nc = tc.nc
+    with (
+        tc.tile_pool(name="held", bufs=1) as held,
+        tc.tile_pool(name="blocks", bufs=2) as blocks,
+    ):
+        offsets = held.tile([P, TOKENS // 16], U16, name="offsets")
+        nc.sync.dma_start(offsets[:], offs)
+
+        weights = held.tile([P, TOKENS], F32, name="weights")
+        nc.vector.memset(weights[:], 1.0 / 3.0)
+        nc.vector.memset(by_sentence(weights[:])[:, :, 0:1], 0.5)
+        nc.vector.memset(by_sentence(weights[:])[:, :, LENGTH - 1 : LENGTH], 0.5)
+
+        for block in range(CHANNELS // P):
+            rows = slice(block * P, (block + 1) * P)
+            tokens = blocks.tile([P, TOKENS], F32, name="tokens")
+            nc.sync.dma_start(tokens[:], x[rows, :])
+            store = blocks.tile([P, SLOTS], F32, name="store")
+            nc.sync.dma_start(store[:], base[rows, :])
+
+            total = blocks.tile([P, TOKENS], F32, name="total")
+            here, summed = by_sentence(tokens[:]), by_sentence(total[:])
+            nc.vector.tensor_tensor(
+                summed[:, :, 0 : LENGTH - 1], here[:, :, 0 : LENGTH - 1], here[:, :, 1:LENGTH], ADD
+            )
+            nc.vector.tensor_copy(summed[:, :, LENGTH - 1 : LENGTH], here[:, :, LENGTH - 1 : LENGTH])
+            nc.vector.tensor_tensor(
+                summed[:, :, 1:LENGTH], summed[:, :, 1:LENGTH], here[:, :, 0 : LENGTH - 1], ADD
+            )
+            pool = blocks.tile([P, TOKENS], F32, name="pool")
+            nc.vector.tensor_tensor(pool[:], total[:], weights[:], MULT)
+
+            nc.vector.tensor_tensor(store[:].indirect(offsets[:]), pool[:], tokens[:], ADD)
+            nc.sync.dma_start(out[rows, :], store[:])

@@ -24,11 +24,6 @@ def tile_synalign_kernel(tc, base, x, offs, out):
         offsets = held.tile([P, TOKENS // 16], U16, name="offsets")
         nc.sync.dma_start(offsets[:], offs)
 
-        weights = held.tile([P, TOKENS], F32, name="weights")
-        nc.vector.memset(weights[:], 1.0 / 3.0)
-        nc.vector.memset(by_sentence(weights[:])[:, :, 0:1], 0.5)
-        nc.vector.memset(by_sentence(weights[:])[:, :, LENGTH - 1 : LENGTH], 0.5)
-
         for block in range(CHANNELS // P):
             rows = slice(block * P, (block + 1) * P)
             tokens = blocks.tile([P, TOKENS], F32, name="tokens")
@@ -36,17 +31,26 @@ def tile_synalign_kernel(tc, base, x, offs, out):
             store = blocks.tile([P, SLOTS], F32, name="store")
             nc.sync.dma_start(store[:], base[rows, :])
 
-            total = blocks.tile([P, TOKENS], F32, name="total")
-            here, summed = by_sentence(tokens[:]), by_sentence(total[:])
+            third = blocks.tile([P, TOKENS], F32, name="third")
+            nc.scalar.mul(third[:], tokens[:], 1.0 / 3.0)
+            half = blocks.tile([P, SENTENCES, 4], F32, name="half")
+            nc.scalar.mul(half[:, :, 0:2], by_sentence(tokens[:])[:, :, 0:2], 0.5)
+            nc.scalar.mul(half[:, :, 2:4], by_sentence(tokens[:])[:, :, LENGTH - 2 : LENGTH], 0.5)
+
+            inner = slice(1, TOKENS - 1)
+            sides = blocks.tile([P, TOKENS], F32, name="sides")
             nc.vector.tensor_tensor(
-                summed[:, :, 0 : LENGTH - 1], here[:, :, 0 : LENGTH - 1], here[:, :, 1:LENGTH], ADD
-            )
-            nc.vector.tensor_copy(summed[:, :, LENGTH - 1 : LENGTH], here[:, :, LENGTH - 1 : LENGTH])
-            nc.vector.tensor_tensor(
-                summed[:, :, 1:LENGTH], summed[:, :, 1:LENGTH], here[:, :, 0 : LENGTH - 1], ADD
+                sides[:, inner], tokens[:, 0 : TOKENS - 2], tokens[:, 2:TOKENS], ADD
             )
             pool = blocks.tile([P, TOKENS], F32, name="pool")
-            nc.vector.tensor_tensor(pool[:], total[:], weights[:], MULT)
+            nc.vector.scalar_tensor_tensor(
+                pool[:, inner], sides[:, inner], 1.0 / 3.0, third[:, inner], MULT, ADD
+            )
+            ends = by_sentence(pool[:])
+            nc.vector.tensor_tensor(ends[:, :, 0:1], half[:, :, 0:1], half[:, :, 1:2], ADD)
+            nc.vector.tensor_tensor(
+                ends[:, :, LENGTH - 1 : LENGTH], half[:, :, 2:3], half[:, :, 3:4], ADD
+            )
 
             nc.vector.tensor_tensor(store[:].indirect(offsets[:]), pool[:], tokens[:], ADD)
             nc.sync.dma_start(out[rows, :], store[:])

@@ -17,40 +17,41 @@ def by_sentence(flat):
 
 def tile_synalign_kernel(tc, base, x, offs, out):
     nc = tc.nc
-    with (
-        tc.tile_pool(name="held", bufs=1) as held,
-        tc.tile_pool(name="blocks", bufs=2) as blocks,
-    ):
+    blocks = range(CHANNELS // P)
+    rows = [slice(b * P, (b + 1) * P) for b in blocks]
+    with tc.tile_pool(name="held", bufs=1) as held:
         offsets = held.tile([P, TOKENS // 16], U16, name="offsets")
         nc.sync.dma_start(offsets[:], offs)
 
-        for block in range(CHANNELS // P):
-            rows = slice(block * P, (block + 1) * P)
-            tokens = blocks.tile([P, TOKENS], F32, name="tokens")
-            nc.sync.dma_start(tokens[:], x[rows, :])
-            store = blocks.tile([P, SLOTS], F32, name="store")
-            nc.sync.dma_start(store[:], base[rows, :])
+        tokens = [held.tile([P, TOKENS], F32, name=f"tokens{b}") for b in blocks]
+        stores = [held.tile([P, SLOTS], F32, name=f"store{b}") for b in blocks]
+        for b in blocks:
+            nc.sync.dma_start(tokens[b][:], x[rows[b], :])
+        for b in blocks:
+            nc.sync.dma_start(stores[b][:], base[rows[b], :])
 
-            third = blocks.tile([P, TOKENS], F32, name="third")
-            nc.scalar.mul(third[:], tokens[:], 1.0 / 3.0)
-            half = blocks.tile([P, SENTENCES, 4], F32, name="half")
-            nc.scalar.mul(half[:, :, 0:2], by_sentence(tokens[:])[:, :, 0:2], 0.5)
-            nc.scalar.mul(half[:, :, 2:4], by_sentence(tokens[:])[:, :, LENGTH - 2 : LENGTH], 0.5)
+        pools = [held.tile([P, TOKENS], F32, name=f"pool{b}") for b in blocks]
+        for b in blocks:
+            third = held.tile([P, TOKENS], F32, name=f"third{b}")
+            nc.scalar.mul(third[:], tokens[b][:], 1.0 / 3.0)
+            half = held.tile([P, SENTENCES, 4], F32, name=f"half{b}")
+            nc.scalar.mul(half[:, :, 0:2], by_sentence(tokens[b][:])[:, :, 0:2], 0.5)
+            nc.scalar.mul(half[:, :, 2:4], by_sentence(tokens[b][:])[:, :, LENGTH - 2 : LENGTH], 0.5)
 
             inner = slice(1, TOKENS - 1)
-            sides = blocks.tile([P, TOKENS], F32, name="sides")
+            sides = held.tile([P, TOKENS], F32, name=f"sides{b}")
             nc.vector.tensor_tensor(
-                sides[:, inner], tokens[:, 0 : TOKENS - 2], tokens[:, 2:TOKENS], ADD
+                sides[:, inner], tokens[b][:, 0 : TOKENS - 2], tokens[b][:, 2:TOKENS], ADD
             )
-            pool = blocks.tile([P, TOKENS], F32, name="pool")
             nc.vector.scalar_tensor_tensor(
-                pool[:, inner], sides[:, inner], 1.0 / 3.0, third[:, inner], MULT, ADD
+                pools[b][:, inner], sides[:, inner], 1.0 / 3.0, third[:, inner], MULT, ADD
             )
-            ends = by_sentence(pool[:])
+            ends = by_sentence(pools[b][:])
             nc.vector.tensor_tensor(ends[:, :, 0:1], half[:, :, 0:1], half[:, :, 1:2], ADD)
             nc.vector.tensor_tensor(
                 ends[:, :, LENGTH - 1 : LENGTH], half[:, :, 2:3], half[:, :, 3:4], ADD
             )
 
-            nc.vector.tensor_tensor(store[:].indirect(offsets[:]), pool[:], tokens[:], ADD)
-            nc.sync.dma_start(out[rows, :], store[:])
+        for b in blocks:
+            nc.vector.tensor_tensor(stores[b][:].indirect(offsets[:]), pools[b][:], tokens[b][:], ADD)
+            nc.sync.dma_start(out[rows[b], :], stores[b][:])

@@ -1,4 +1,5 @@
 import concourse.mybir as mybir
+from concourse.masks import make_identity
 
 F32 = mybir.dt.float32
 U16 = mybir.dt.uint16
@@ -9,6 +10,8 @@ P = 128
 CHANNELS, SLOTS = 256, 4096
 SENTENCES, LENGTH = 8, 128
 TOKENS = SENTENCES * LENGTH
+GROUP = 4
+EARLY = 4
 
 
 def by_sentence(flat):
@@ -19,38 +22,59 @@ def tile_synalign_kernel(tc, base, x, offs, out):
     nc = tc.nc
     blocks = range(CHANNELS // P)
     rows = [slice(b * P, (b + 1) * P) for b in blocks]
-    with tc.tile_pool(name="held", bufs=1) as held:
+    with (
+        tc.tile_pool(name="held", bufs=1) as held,
+        tc.psum_pool(name="sums", bufs=1) as sums,
+    ):
         offsets = held.tile([P, TOKENS // 16], U16, name="offsets")
         nc.sync.dma_start(offsets[:], offs)
 
         tokens = [held.tile([P, TOKENS], F32, name=f"tokens{b}") for b in blocks]
         stores = [held.tile([P, SLOTS], F32, name=f"store{b}") for b in blocks]
-        for b in blocks:
-            nc.sync.dma_start(tokens[b][:], x[rows[b], :])
-        for b in blocks:
-            nc.sync.dma_start(stores[b][:], base[rows[b], :])
+        split = EARLY * LENGTH
+        nc.sync.dma_start(tokens[0][:], x[rows[0], :])
+        nc.sync.dma_start(tokens[1][:, 0:split], x[rows[1], 0:split])
+        nc.sync.dma_start(stores[0][:], base[rows[0], :])
+        nc.sync.dma_start(tokens[1][:, split:TOKENS], x[rows[1], split:TOKENS])
+        nc.sync.dma_start(stores[1][:], base[rows[1], :])
+
+        identity = held.tile([P, P], F32, name="identity")
+        make_identity(nc, identity[:])
 
         pools = [held.tile([P, TOKENS], F32, name=f"pool{b}") for b in blocks]
-        for b in blocks:
-            third = held.tile([P, TOKENS], F32, name=f"third{b}")
-            nc.scalar.mul(third[:], tokens[b][:], 1.0 / 3.0)
-            half = held.tile([P, SENTENCES, 4], F32, name=f"half{b}")
-            nc.scalar.mul(half[:, :, 0:2], by_sentence(tokens[b][:])[:, :, 0:2], 0.5)
-            nc.scalar.mul(half[:, :, 2:4], by_sentence(tokens[b][:])[:, :, LENGTH - 2 : LENGTH], 0.5)
+        last = LENGTH - 1
 
-            inner = slice(1, TOKENS - 1)
-            sides = held.tile([P, TOKENS], F32, name=f"sides{b}")
-            nc.vector.tensor_tensor(
-                sides[:, inner], tokens[b][:, 0 : TOKENS - 2], tokens[b][:, 2:TOKENS], ADD
+        third = held.tile([P, TOKENS], F32, name="third")
+        nc.scalar.mul(third[:], tokens[0][:], 1.0 / 3.0)
+        half = held.tile([P, SENTENCES, 4], F32, name="half")
+        nc.scalar.mul(half[:, :, 0:2], by_sentence(tokens[0][:])[:, :, 0:2], 0.5)
+        nc.scalar.mul(half[:, :, 2:4], by_sentence(tokens[0][:])[:, :, last - 1 : LENGTH], 0.5)
+        inner = slice(1, TOKENS - 1)
+        sides = held.tile([P, TOKENS], F32, name="sides")
+        nc.vector.tensor_tensor(
+            sides[:, inner], tokens[0][:, 0 : TOKENS - 2], tokens[0][:, 2:TOKENS], ADD
+        )
+        nc.vector.scalar_tensor_tensor(
+            pools[0][:, inner], sides[:, inner], 1.0 / 3.0, third[:, inner], MULT, ADD
+        )
+        ends = by_sentence(pools[0][:])
+        nc.vector.tensor_tensor(ends[:, :, 0:1], half[:, :, 0:1], half[:, :, 1:2], ADD)
+        nc.vector.tensor_tensor(ends[:, :, last:LENGTH], half[:, :, 2:3], half[:, :, 3:4], ADD)
+
+        for first in range(0, SENTENCES, GROUP):
+            group = by_sentence(tokens[1][:])[:, first : first + GROUP, :]
+            total = sums.tile([P, GROUP, LENGTH], F32, name=f"total{first}")
+            nc.tensor.matmul(total[:], identity[:], group, start=True, stop=False)
+            nc.tensor.matmul(
+                total[:, :, 1:LENGTH], identity[:], group[:, :, 0:last], start=False, stop=False
             )
-            nc.vector.scalar_tensor_tensor(
-                pools[b][:, inner], sides[:, inner], 1.0 / 3.0, third[:, inner], MULT, ADD
+            nc.tensor.matmul(
+                total[:, :, 0:last], identity[:], group[:, :, 1:LENGTH], start=False, stop=True
             )
-            ends = by_sentence(pools[b][:])
-            nc.vector.tensor_tensor(ends[:, :, 0:1], half[:, :, 0:1], half[:, :, 1:2], ADD)
-            nc.vector.tensor_tensor(
-                ends[:, :, LENGTH - 1 : LENGTH], half[:, :, 2:3], half[:, :, 3:4], ADD
-            )
+            pooled = by_sentence(pools[1][:])[:, first : first + GROUP, :]
+            nc.scalar.mul(pooled[:, :, 1:last], total[:, :, 1:last], 1.0 / 3.0)
+            nc.scalar.mul(pooled[:, :, 0:1], total[:, :, 0:1], 0.5)
+            nc.scalar.mul(pooled[:, :, last:LENGTH], total[:, :, last:LENGTH], 0.5)
 
         for b in blocks:
             nc.vector.tensor_tensor(stores[b][:].indirect(offsets[:]), pools[b][:], tokens[b][:], ADD)

@@ -10,8 +10,8 @@ P = 128
 CHANNELS, SLOTS = 256, 4096
 SENTENCES, LENGTH = 8, 128
 TOKENS = SENTENCES * LENGTH
-GROUP = 4
-EARLY = 4
+GROUP = 2
+EARLY = 2
 
 
 def by_sentence(flat):

@@ -12,6 +12,7 @@ SENTENCES, LENGTH = 8, 128
 TOKENS = SENTENCES * LENGTH
 GROUP = 2
 EARLY = 2
+ON_VECTOR = 6
 
 
 def by_sentence(flat):
@@ -44,26 +45,29 @@ def tile_synalign_kernel(tc, base, x, offs, out):
         pools = [held.tile([P, TOKENS], F32, name=f"pool{b}") for b in blocks]
         last = LENGTH - 1
 
-        third = held.tile([P, TOKENS], F32, name="third")
-        nc.scalar.mul(third[:], tokens[0][:], 1.0 / 3.0)
-        half = held.tile([P, SENTENCES, 4], F32, name="half")
-        nc.scalar.mul(half[:, :, 0:2], by_sentence(tokens[0][:])[:, :, 0:2], 0.5)
-        nc.scalar.mul(half[:, :, 2:4], by_sentence(tokens[0][:])[:, :, last - 1 : LENGTH], 0.5)
-        inner = slice(1, TOKENS - 1)
-        sides = held.tile([P, TOKENS], F32, name="sides")
+        width = ON_VECTOR * LENGTH
+        third = held.tile([P, width], F32, name="third")
+        nc.scalar.mul(third[:], tokens[0][:, 0:width], 1.0 / 3.0)
+        half = held.tile([P, ON_VECTOR, 4], F32, name="half")
+        nc.scalar.mul(half[:, :, 0:2], by_sentence(tokens[0][:, 0:width])[:, :, 0:2], 0.5)
+        nc.scalar.mul(half[:, :, 2:4], by_sentence(tokens[0][:, 0:width])[:, :, last - 1 : LENGTH], 0.5)
+        inner = slice(1, width - 1)
+        sides = held.tile([P, width], F32, name="sides")
         nc.vector.tensor_tensor(
-            sides[:, inner], tokens[0][:, 0 : TOKENS - 2], tokens[0][:, 2:TOKENS], ADD
+            sides[:, inner], tokens[0][:, 0 : width - 2], tokens[0][:, 2:width], ADD
         )
         nc.vector.scalar_tensor_tensor(
             pools[0][:, inner], sides[:, inner], 1.0 / 3.0, third[:, inner], MULT, ADD
         )
-        ends = by_sentence(pools[0][:])
+        ends = by_sentence(pools[0][:, 0:width])
         nc.vector.tensor_tensor(ends[:, :, 0:1], half[:, :, 0:1], half[:, :, 1:2], ADD)
         nc.vector.tensor_tensor(ends[:, :, last:LENGTH], half[:, :, 2:3], half[:, :, 3:4], ADD)
 
-        for first in range(0, SENTENCES, GROUP):
-            group = by_sentence(tokens[1][:])[:, first : first + GROUP, :]
-            total = sums.tile([P, GROUP, LENGTH], F32, name=f"total{first}")
+        groups = [(0, first) for first in range(ON_VECTOR, SENTENCES, GROUP)]
+        groups += [(1, first) for first in range(0, SENTENCES, GROUP)]
+        for b, first in groups:
+            group = by_sentence(tokens[b][:])[:, first : first + GROUP, :]
+            total = sums.tile([P, GROUP, LENGTH], F32, name=f"total{b}_{first}")
             nc.tensor.matmul(total[:], identity[:], group, start=True, stop=False)
             nc.tensor.matmul(
                 total[:, :, 1:LENGTH], identity[:], group[:, :, 0:last], start=False, stop=False
@@ -71,7 +75,7 @@ def tile_synalign_kernel(tc, base, x, offs, out):
             nc.tensor.matmul(
                 total[:, :, 0:last], identity[:], group[:, :, 1:LENGTH], start=False, stop=True
             )
-            pooled = by_sentence(pools[1][:])[:, first : first + GROUP, :]
+            pooled = by_sentence(pools[b][:])[:, first : first + GROUP, :]
             nc.scalar.mul(pooled[:, :, 1:last], total[:, :, 1:last], 1.0 / 3.0)
             nc.scalar.mul(pooled[:, :, 0:1], total[:, :, 0:1], 0.5)
             nc.scalar.mul(pooled[:, :, last:LENGTH], total[:, :, last:LENGTH], 0.5)

@@ -5,14 +5,14 @@ F32 = mybir.dt.float32
 U16 = mybir.dt.uint16
 ADD = mybir.AluOpType.add
 MULT = mybir.AluOpType.mult
+IS_GE = mybir.AluOpType.is_ge
 
 P = 128
 CHANNELS, SLOTS = 256, 4096
 SENTENCES, LENGTH = 8, 128
 TOKENS = SENTENCES * LENGTH
 GROUP = 2
-EARLY = 2
-ON_VECTOR = 6
+BANK = 4
 
 
 def by_sentence(flat):
@@ -25,60 +25,70 @@ def tile_synalign_kernel(tc, base, x, offs, out):
     rows = [slice(b * P, (b + 1) * P) for b in blocks]
     with (
         tc.tile_pool(name="held", bufs=1) as held,
-        tc.psum_pool(name="sums", bufs=1) as sums,
+        tc.psum_pool(name="banks", bufs=1) as banks,
     ):
         offsets = held.tile([P, TOKENS // 16], U16, name="offsets")
         nc.sync.dma_start(offsets[:], offs)
 
         tokens = [held.tile([P, TOKENS], F32, name=f"tokens{b}") for b in blocks]
         stores = [held.tile([P, SLOTS], F32, name=f"store{b}") for b in blocks]
-        split = EARLY * LENGTH
-        nc.sync.dma_start(tokens[0][:], x[rows[0], :])
-        nc.sync.dma_start(tokens[1][:, 0:split], x[rows[1], 0:split])
-        nc.sync.dma_start(stores[0][:], base[rows[0], :])
-        nc.sync.dma_start(tokens[1][:, split:TOKENS], x[rows[1], split:TOKENS])
-        nc.sync.dma_start(stores[1][:], base[rows[1], :])
+        for b in blocks:
+            nc.sync.dma_start(tokens[b][:], x[rows[b], :])
+            nc.sync.dma_start(stores[b][:], base[rows[b], :])
 
         identity = held.tile([P, P], F32, name="identity")
         make_identity(nc, identity[:])
-
-        pools = [held.tile([P, TOKENS], F32, name=f"pool{b}") for b in blocks]
         last = LENGTH - 1
 
-        width = ON_VECTOR * LENGTH
-        third = held.tile([P, width], F32, name="third")
-        nc.scalar.mul(third[:], tokens[0][:, 0:width], 1.0 / 3.0)
-        half = held.tile([P, ON_VECTOR, 4], F32, name="half")
-        nc.scalar.mul(half[:, :, 0:2], by_sentence(tokens[0][:, 0:width])[:, :, 0:2], 0.5)
-        nc.scalar.mul(half[:, :, 2:4], by_sentence(tokens[0][:, 0:width])[:, :, last - 1 : LENGTH], 0.5)
-        inner = slice(1, width - 1)
-        sides = held.tile([P, width], F32, name="sides")
+        window_sum = held.tile([P, LENGTH], F32, name="window_sum")
+        nc.gpsimd.memset(window_sum[:], 1.0)
+        nc.gpsimd.memset(window_sum[:, 0:1], 1.5)
+        nc.gpsimd.memset(window_sum[:, last:LENGTH], 1.5)
+        for sign in (1, -1):
+            nc.gpsimd.affine_select(
+                out=window_sum[:],
+                in_=window_sum[:],
+                pattern=[[sign, LENGTH]],
+                compare_op=IS_GE,
+                fill=0.0,
+                base=1,
+                channel_multiplier=-sign,
+            )
+
+        pools = [held.tile([P, TOKENS], F32, name=f"pool{b}") for b in blocks]
+
+        third = held.tile([P, TOKENS], F32, name="third")
+        nc.scalar.mul(third[:], tokens[0][:], 1.0 / 3.0)
+        half = held.tile([P, SENTENCES, 4], F32, name="half")
+        nc.scalar.mul(half[:, :, 0:2], by_sentence(tokens[0][:])[:, :, 0:2], 0.5)
+        nc.scalar.mul(half[:, :, 2:4], by_sentence(tokens[0][:])[:, :, last - 1 : LENGTH], 0.5)
+        inner = slice(1, TOKENS - 1)
+        sides = held.tile([P, TOKENS], F32, name="sides")
         nc.vector.tensor_tensor(
-            sides[:, inner], tokens[0][:, 0 : width - 2], tokens[0][:, 2:width], ADD
+            sides[:, inner], tokens[0][:, 0 : TOKENS - 2], tokens[0][:, 2:TOKENS], ADD
         )
         nc.vector.scalar_tensor_tensor(
             pools[0][:, inner], sides[:, inner], 1.0 / 3.0, third[:, inner], MULT, ADD
         )
-        ends = by_sentence(pools[0][:, 0:width])
+        ends = by_sentence(pools[0][:])
         nc.vector.tensor_tensor(ends[:, :, 0:1], half[:, :, 0:1], half[:, :, 1:2], ADD)
         nc.vector.tensor_tensor(ends[:, :, last:LENGTH], half[:, :, 2:3], half[:, :, 3:4], ADD)
 
-        groups = [(0, first) for first in range(ON_VECTOR, SENTENCES, GROUP)]
-        groups += [(1, first) for first in range(0, SENTENCES, GROUP)]
-        for b, first in groups:
-            group = by_sentence(tokens[b][:])[:, first : first + GROUP, :]
-            total = sums.tile([P, GROUP, LENGTH], F32, name=f"total{b}_{first}")
-            nc.tensor.matmul(total[:], identity[:], group, start=True, stop=False)
-            nc.tensor.matmul(
-                total[:, :, 1:LENGTH], identity[:], group[:, :, 0:last], start=False, stop=False
-            )
-            nc.tensor.matmul(
-                total[:, :, 0:last], identity[:], group[:, :, 1:LENGTH], start=False, stop=True
-            )
-            pooled = by_sentence(pools[b][:])[:, first : first + GROUP, :]
-            nc.scalar.mul(pooled[:, :, 1:last], total[:, :, 1:last], 1.0 / 3.0)
-            nc.scalar.mul(pooled[:, :, 0:1], total[:, :, 0:1], 0.5)
-            nc.scalar.mul(pooled[:, :, last:LENGTH], total[:, :, last:LENGTH], 0.5)
+        cuts = [slice(first, first + GROUP) for first in range(0, SENTENCES, GROUP)]
+        turned = held.tile([P, SENTENCES, P], F32, name="turned")
+        for cut in cuts:
+            turned_bank = banks.tile([P, BANK, P], F32, name="turned_bank", bufs=len(cuts))
+            for s in range(GROUP):
+                sentence = by_sentence(tokens[1][:])[:, cut.start + s, :]
+                nc.tensor.transpose(turned_bank[:, s, :], sentence, identity[:])
+            nc.scalar.copy(turned[:, cut, :], turned_bank[:, 0:GROUP, :])
+        for cut in cuts:
+            banded = banks.tile([P, BANK, LENGTH], F32, name="banded", bufs=3)
+            for s in range(GROUP):
+                nc.tensor.matmul(
+                    banded[:, s, :], turned[:, cut.start + s, :], window_sum[:], start=True, stop=True
+                )
+            nc.scalar.mul(by_sentence(pools[1][:])[:, cut, :], banded[:, 0:GROUP, :], 1.0 / 3.0)
 
         for b in blocks:
             nc.vector.tensor_tensor(stores[b][:].indirect(offsets[:]), pools[b][:], tokens[b][:], ADD)

@@ -32,9 +32,12 @@ def tile_synalign_kernel(tc, base, x, offs, out):
 
         tokens = [held.tile([P, TOKENS], F32, name=f"tokens{b}") for b in blocks]
         stores = [held.tile([P, SLOTS], F32, name=f"store{b}") for b in blocks]
-        for b in blocks:
-            nc.sync.dma_start(tokens[b][:], x[rows[b], :])
-            nc.sync.dma_start(stores[b][:], base[rows[b], :])
+        middle = TOKENS // 2
+        nc.sync.dma_start(tokens[0][:], x[rows[0], :])
+        nc.sync.dma_start(stores[0][:], base[rows[0], :])
+        for half_row in (slice(0, middle), slice(middle, TOKENS)):
+            nc.sync.dma_start(tokens[1][:, half_row], x[rows[1], half_row])
+        nc.sync.dma_start(stores[1][:], base[rows[1], :])
 
         identity = held.tile([P, P], F32, name="identity")
         make_identity(nc, identity[:])

@@ -1,11 +1,11 @@
 import concourse.mybir as mybir
-from concourse.masks import make_identity
 
 F32 = mybir.dt.float32
 U16 = mybir.dt.uint16
 ADD = mybir.AluOpType.add
 MULT = mybir.AluOpType.mult
-IS_GE = mybir.AluOpType.is_ge
+IS_EQUAL = mybir.AluOpType.is_equal
+IS_LE = mybir.AluOpType.is_le
 
 P = 128
 CHANNELS, SLOTS = 256, 4096
@@ -39,24 +39,22 @@ def tile_synalign_kernel(tc, base, x, offs, out):
             nc.sync.dma_start(tokens[1][:, half_row], x[rows[1], half_row])
         nc.sync.dma_start(stores[1][:], base[rows[1], :])
 
-        identity = held.tile([P, P], F32, name="identity")
-        make_identity(nc, identity[:])
         last = LENGTH - 1
-
+        distance = held.tile([P, LENGTH], F32, name="distance")
+        nc.gpsimd.iota(
+            distance[:],
+            pattern=[[1, LENGTH]],
+            base=0,
+            channel_multiplier=-1,
+            allow_small_or_imprecise_dtypes=True,
+        )
+        identity = held.tile([P, P], F32, name="identity")
+        nc.gpsimd.tensor_scalar(identity[:], distance[:], 0.0, None, IS_EQUAL)
         window_sum = held.tile([P, LENGTH], F32, name="window_sum")
-        nc.gpsimd.memset(window_sum[:], 1.0)
-        nc.gpsimd.memset(window_sum[:, 0:1], 1.5)
-        nc.gpsimd.memset(window_sum[:, last:LENGTH], 1.5)
-        for sign in (1, -1):
-            nc.gpsimd.affine_select(
-                out=window_sum[:],
-                in_=window_sum[:],
-                pattern=[[sign, LENGTH]],
-                compare_op=IS_GE,
-                fill=0.0,
-                base=1,
-                channel_multiplier=-sign,
-            )
+        nc.gpsimd.tensor_tensor(window_sum[:], distance[:], distance[:], MULT)
+        nc.gpsimd.tensor_scalar(window_sum[:], window_sum[:], 1.0, None, IS_LE)
+        both_ends = window_sum[:, 0:LENGTH:last]
+        nc.gpsimd.tensor_scalar_mul(both_ends, both_ends, 1.5)
 
         pools = [held.tile([P, TOKENS], F32, name=f"pool{b}") for b in blocks]
 

@@ -28,13 +28,12 @@ def tile_synalign_kernel(tc, base, x, offs, out):
         tc.psum_pool(name="banks", bufs=1) as banks,
     ):
         offsets = held.tile([P, TOKENS // 16], U16, name="offsets")
-        nc.sync.dma_start(offsets[:], offs)
-
         tokens = [held.tile([P, TOKENS], F32, name=f"tokens{b}") for b in blocks]
         stores = [held.tile([P, SLOTS], F32, name=f"store{b}") for b in blocks]
         middle = TOKENS // 2
         nc.sync.dma_start(tokens[0][:], x[rows[0], :])
         nc.sync.dma_start(stores[0][:], base[rows[0], :])
+        nc.sync.dma_start(offsets[:], offs)
         for half_row in (slice(0, middle), slice(middle, TOKENS)):
             nc.sync.dma_start(tokens[1][:, half_row], x[rows[1], half_row])
         nc.sync.dma_start(stores[1][:], base[rows[1], :])

import concourse.mybir as mybir

F32 = mybir.dt.float32
U16 = mybir.dt.uint16
ADD = mybir.AluOpType.add
MULT = mybir.AluOpType.mult
IS_EQUAL = mybir.AluOpType.is_equal
IS_LE = mybir.AluOpType.is_le

P = 128
CHANNELS, SLOTS = 256, 4096
SENTENCES, LENGTH = 8, 128
TOKENS = SENTENCES * LENGTH
GROUP = 2
BANK = 4


def by_sentence(flat):
    return flat.rearrange("p (s t) -> p s t", t=LENGTH)


def tile_synalign_kernel(tc, base, x, offs, out):
    nc = tc.nc
    blocks = range(CHANNELS // P)
    rows = [slice(b * P, (b + 1) * P) for b in blocks]
    with (
        tc.tile_pool(name="held", bufs=1) as held,
        tc.psum_pool(name="banks", bufs=1) as banks,
    ):
        offsets = held.tile([P, TOKENS // 16], U16, name="offsets")
        tokens = [held.tile([P, TOKENS], F32, name=f"tokens{b}") for b in blocks]
        stores = [held.tile([P, SLOTS], F32, name=f"store{b}") for b in blocks]
        middle = TOKENS // 2
        nc.sync.dma_start(tokens[0][:], x[rows[0], :])
        nc.sync.dma_start(stores[0][:], base[rows[0], :])
        nc.sync.dma_start(offsets[:], offs)
        for half_row in (slice(0, middle), slice(middle, TOKENS)):
            nc.sync.dma_start(tokens[1][:, half_row], x[rows[1], half_row])
        nc.sync.dma_start(stores[1][:], base[rows[1], :])

        last = LENGTH - 1
        distance = held.tile([P, LENGTH], F32, name="distance")
        nc.gpsimd.iota(
            distance[:],
            pattern=[[1, LENGTH]],
            base=0,
            channel_multiplier=-1,
            allow_small_or_imprecise_dtypes=True,
        )
        identity = held.tile([P, P], F32, name="identity")
        nc.gpsimd.tensor_scalar(identity[:], distance[:], 0.0, None, IS_EQUAL)
        window_sum = held.tile([P, LENGTH], F32, name="window_sum")
        nc.gpsimd.tensor_tensor(window_sum[:], distance[:], distance[:], MULT)
        nc.gpsimd.tensor_scalar(window_sum[:], window_sum[:], 1.0, None, IS_LE)
        both_ends = window_sum[:, 0:LENGTH:last]
        nc.gpsimd.tensor_scalar_mul(both_ends, both_ends, 1.5)

        pools = [held.tile([P, TOKENS], F32, name=f"pool{b}") for b in blocks]

        third = held.tile([P, TOKENS], F32, name="third")
        nc.scalar.mul(third[:], tokens[0][:], 1.0 / 3.0)
        half = held.tile([P, SENTENCES, 4], F32, name="half")
        nc.scalar.mul(half[:, :, 0:2], by_sentence(tokens[0][:])[:, :, 0:2], 0.5)
        nc.scalar.mul(half[:, :, 2:4], by_sentence(tokens[0][:])[:, :, last - 1 : LENGTH], 0.5)
        inner = slice(1, TOKENS - 1)
        sides = held.tile([P, TOKENS], F32, name="sides")
        nc.vector.tensor_tensor(
            sides[:, inner], tokens[0][:, 0 : TOKENS - 2], tokens[0][:, 2:TOKENS], ADD
        )
        nc.vector.scalar_tensor_tensor(
            pools[0][:, inner], sides[:, inner], 1.0 / 3.0, third[:, inner], MULT, ADD
        )
        ends = by_sentence(pools[0][:])
        nc.vector.tensor_tensor(ends[:, :, 0:1], half[:, :, 0:1], half[:, :, 1:2], ADD)
        nc.vector.tensor_tensor(ends[:, :, last:LENGTH], half[:, :, 2:3], half[:, :, 3:4], ADD)

        cuts = [slice(first, first + GROUP) for first in range(0, SENTENCES, GROUP)]
        turned = held.tile([P, SENTENCES, P], F32, name="turned")
        for cut in cuts:
            turned_bank = banks.tile([P, BANK, P], F32, name="turned_bank", bufs=len(cuts))
            for s in range(GROUP):
                sentence = by_sentence(tokens[1][:])[:, cut.start + s, :]
                nc.tensor.transpose(turned_bank[:, s, :], sentence, identity[:])
            nc.scalar.copy(turned[:, cut, :], turned_bank[:, 0:GROUP, :])
        for cut in cuts:
            banded = banks.tile([P, BANK, LENGTH], F32, name="banded", bufs=3)
            for s in range(GROUP):
                nc.tensor.matmul(
                    banded[:, s, :], turned[:, cut.start + s, :], window_sum[:], start=True, stop=True
                )
            nc.scalar.mul(by_sentence(pools[1][:])[:, cut, :], banded[:, 0:GROUP, :], 1.0 / 3.0)

        for b in blocks:
            nc.vector.tensor_tensor(stores[b][:].indirect(offsets[:]), pools[b][:], tokens[b][:], ADD)
            nc.sync.dma_start(out[rows[b], :], stores[b][:])
